import numpy as np
import ml_dtypes


def mxq(x, axis, fmt="e4m3"):
    dtype, down = {"e4m3": (ml_dtypes.float8_e4m3fn, 7), "e5m2": (ml_dtypes.float8_e5m2, 14)}[fmt]
    v = np.moveaxis(np.asarray(x, np.float32).astype(ml_dtypes.bfloat16).astype(np.float64), axis, -1)
    blocks = v.reshape(v.shape[:-1] + (-1, 32))
    amax = np.abs(blocks).max(-1, keepdims=True)
    byte = np.maximum(np.where(amax > 0, np.frexp(amax)[1] - 1 + 127, 0) - down, 1)
    scale = np.exp2(byte - 127.0)
    codes = (blocks / scale).astype(np.float32).astype(dtype).astype(np.float64)
    return np.moveaxis((codes * scale).reshape(v.shape), -1, axis)


WIDE = False


def mx_kscale(k):
    if not WIDE:
        return np.ones(k)
    levels = np.array([10, -10, 5, -5, 0])
    a = np.random.permutation(np.resize(levels, k // 512 * 4)).reshape(k // 512, 4)
    idx = np.arange(k)
    return np.exp2(a[idx // 512, idx % 128 // 32])


BF16 = ml_dtypes.bfloat16


def bf(x):
    return np.asarray(x, np.float32).astype(BF16)


def f64(x):
    return np.asarray(x).astype(np.float64)


E2M1 = np.array([0.0, 0.5, 1.0, 1.5, 2.0, 3.0, 4.0, 6.0, -0.0, -0.5, -1.0, -1.5, -2.0, -3.0, -4.0, -6.0])


def pack_weight(w, fmt):
    k, n = w.shape
    w = f64(bf(w)).reshape(k // 32, 32, n)
    amax = np.abs(w).max(1)
    if fmt == "e4m3":
        byte = np.frexp(amax)[1] - 1 + 127 - 7
    else:
        mant, ex = np.frexp(amax / 6.0)
        byte = np.where(mant > 0.5, ex, ex - 1) + 127
    byte = np.clip(np.where(amax > 0, byte, 1), 1, 254)
    scaled = (w * np.exp2(127.0 - byte)[:, None, :]).reshape(k, n).astype(np.float32)
    by_word = np.ascontiguousarray(scaled.reshape(k // 512, 128, 4, n).transpose(0, 1, 3, 2))
    if fmt == "e4m3":
        words = by_word.astype(ml_dtypes.float8_e4m3fn).view(np.uint8)
    else:
        c = by_word.astype(ml_dtypes.float4_e2m1fn).view(np.uint8) & 0xF
        words = c[..., 0::2] | (c[..., 1::2] << 4)
    return np.ascontiguousarray(words), np.ascontiguousarray(byte.astype(np.uint8).reshape(k // 512, 16, n))


def unpack_weight(words, scales, fmt):
    g, p, n, _ = words.shape
    if fmt == "e4m3":
        vals = np.ascontiguousarray(words).view(ml_dtypes.float8_e4m3fn).astype(np.float64)
    else:
        nib = np.empty((g, p, n, 4), np.uint8)
        nib[..., 0::2] = words & 0xF
        nib[..., 1::2] = words >> 4
        vals = E2M1[nib]
    vals = vals * np.repeat(np.exp2(scales.astype(np.float64) - 127.0), 8, axis=1)[..., None]
    return vals.transpose(0, 1, 3, 2).reshape(g * 512, n)


B, N, DIM, HEADS, DIM_HEAD = 2, 64, 4096, 24, 64
INNER = HEADS * DIM_HEAD
FMT = "e4m3"


def setup_inputs():
    s = mx_kscale(DIM)
    x = bf(np.random.standard_normal((B, N, DIM)) * s)
    w = np.random.standard_normal((3 * INNER, DIM)) / np.sqrt(DIM) / s[None, :]
    words, scales = pack_weight(np.ascontiguousarray(w.T), FMT)
    return {"x": x, "W_words": words, "W_scales": scales}


def reference(x, W_words, W_scales):
    b, n, _ = x.shape
    qkv = mxq(f64(x), 2, "e4m3") @ unpack_weight(W_words, W_scales, FMT)
    q, k, v = np.split(qkv, 3, axis=-1)

    def to_heads(t):
        return t.reshape(b, n, HEADS, DIM_HEAD).transpose(0, 2, 1, 3)

    return to_heads(q), to_heads(k), to_heads(v)

@@ -1,0 +1,124 @@
+import concourse.mybir as mybir
+from concourse.masks import make_identity
+
+F32 = mybir.dt.float32
+BF16 = mybir.dt.bfloat16
+U8 = mybir.dt.uint8
+U32 = mybir.dt.uint32
+I32 = mybir.dt.int32
+FP8X4 = mybir.dt.float8_e4m3fn_x4
+
+P = 128
+TOKENS = 128
+DIM = 4096
+COLS = 4608
+GROUPS = 8
+N_TILE = 512
+TILES = COLS // N_TILE
+TILES_A = 4
+COLS_A = TILES_A * N_TILE
+COLS_B = COLS - COLS_A
+HEADS_PER_TILE = 8
+TILES_PER_OUT = 3
+
+FLOPS = 2 * TOKENS * DIM * COLS
+
+
+def tile_get_qkv_w_kernel(tc, x, W_words, W_scales, out_0, out_1, out_2):
+    nc = tc.nc
+    outs = [out_0, out_1, out_2]
+    with tc.tile_pool(name="keep", bufs=1) as keep, tc.psum_pool(name="psum", bufs=8) as psum, tc.manual_schedule():
+        planes = keep.tile([P, 2 * COLS], U8, align_bytes=64)
+        x_sb = keep.tile([P, DIM], BF16, align_bytes=64)
+        grouped = keep.tile([P, DIM], BF16, align_bytes=64)
+        x_codes = keep.tile([P, GROUPS * TOKENS], U32, align_bytes=64)
+        x_scales = keep.tile([P, GROUPS * TOKENS], U8, align_bytes=64)
+        ident = keep.tile([P, P], F32)
+        w_a = [keep.tile([P, COLS_A], U32, align_bytes=64, name="w_a%d" % g) for g in range(GROUPS)]
+        w_b = [keep.tile([P, COLS_B], U32, align_bytes=64, name="w_b%d" % g) for g in range(GROUPS)]
+        stage = [keep.tile([P, TILES_PER_OUT * N_TILE], F32, name="stage%d" % o) for o in range(3)]
+
+        nc.vector.memset(planes[:].bitcast(I32), 0)
+        make_identity(nc, ident[:])
+
+        for b in range(2):
+            nc.sync.dma_start(out=x_sb[b:P:2, :], in_=x[b])
+        for half in range(2):
+            for q in range(4):
+                nc.sync.dma_start(
+                    out=planes[32 * q : 32 * q + 16, COLS * half : COLS * (half + 1)].bitcast(I32),
+                    in_=W_scales[4 * half : 4 * half + 4, 4 * q : 4 * q + 4, :].bitcast(I32),
+                )
+        for g in range(GROUPS):
+            src = W_words[g].rearrange("p n t -> p (n t)")
+            nc.sync.dma_start(out=w_a[g][:].bitcast(I32), in_=src[:, 0 : 4 * COLS_A].bitcast(I32))
+        for g in range(GROUPS):
+            src = W_words[g].rearrange("p n t -> p (n t)")
+            nc.sync.dma_start(out=w_b[g][:].bitcast(I32), in_=src[:, 4 * COLS_A : 4 * COLS].bitcast(I32))
+
+        x_words = x_sb[:].bitcast(F32)
+        grouped_words = grouped[:].bitcast(F32)
+        for a in range(4):
+            xt = psum.tile([P, 4, TOKENS], F32, tag="bank", name="xt%d" % a)
+            for gg in range(2):
+                for u in range(2):
+                    g = 2 * a + gg
+                    nc.tensor.transpose(xt[:, 2 * gg + u, :], x_words[:, 256 * g + u : 256 * (g + 1) : 2], ident[:])
+            dst = grouped_words[:, 512 * a : 512 * (a + 1)].rearrange("p (g t u) -> p g t u", g=2, u=2)
+            view = xt[:].rearrange("p (g u) t -> p g t u", u=2)
+            if a % 2 == 0:
+                nc.vector.tensor_copy(out=dst, in_=view)
+            else:
+                nc.scalar.copy(out=dst, in_=view)
+        for hq in range(2):
+            nc.vector.quantize_mx(
+                out=x_codes[:, 512 * hq : 512 * (hq + 1)].bitcast(FP8X4),
+                scales=x_scales[:, 512 * hq : 512 * (hq + 1)],
+                in_=grouped[:, 2048 * hq : 2048 * (hq + 1)],
+            )
+
+        acc = {}
+
+        def one_pass(g, t):
+            if t < TILES_A:
+                words = w_a[g][:, N_TILE * t : N_TILE * (t + 1)]
+            else:
+                words = w_b[g][:, N_TILE * (t - TILES_A) : N_TILE * (t - TILES_A + 1)]
+            k = 4 * (g % 4)
+            c0 = COLS * (g // 4) + N_TILE * t
+            nc.tensor.matmul_mx(
+                out=acc[t][:],
+                lhsT=x_codes[:, TOKENS * g : TOKENS * (g + 1)].bitcast(FP8X4),
+                lhsT_scale=x_scales[:, TOKENS * g : TOKENS * (g + 1)],
+                rhs=words.bitcast(FP8X4),
+                rhs_scale=planes[k:P, c0 : c0 + N_TILE],
+                start=(g == 0),
+                stop=(g == GROUPS - 1),
+            )
+
+        def leave(t):
+            o, part = divmod(t, TILES_PER_OUT)
+            dst = stage[o][:, N_TILE * part : N_TILE * (part + 1)]
+            if t % 2 == 0:
+                nc.scalar.copy(out=dst, in_=acc[t][:])
+            else:
+                nc.vector.tensor_copy(out=dst, in_=acc[t][:])
+
+        def store(t):
+            o, part = divmod(t, TILES_PER_OUT)
+            for b in range(2):
+                nc.sync.dma_start(
+                    out=outs[o][b, HEADS_PER_TILE * part : HEADS_PER_TILE * (part + 1), :, :].rearrange("h n d -> n h d"),
+                    in_=stage[o][b:P:2, N_TILE * part : N_TILE * (part + 1)].rearrange("p (h d) -> p h d", h=HEADS_PER_TILE),
+                )
+
+        for tiles in (list(range(0, TILES_A)), list(range(TILES_A, TILES))):
+            for t in tiles:
+                acc[t] = psum.tile([P, N_TILE], F32, tag="bank", name="acc%d" % t)
+            for g in range(GROUPS):
+                for t in tiles:
+                    one_pass(g, t)
+                    if g == GROUPS - 1:
+                        leave(t)
+        for t in range(TILES):
+            store(t)

@@ -45,9 +45,9 @@ def tile_get_qkv_w_kernel(tc, x, W_words, W_scales, out_0, out_1, out_2):
             nc.sync.dma_start(out=x_sb[b:P:2, :], in_=x[b])
         for half in range(2):
             for q in range(4):
-                nc.sync.dma_start(
-                    out=planes[32 * q : 32 * q + 16, COLS * half : COLS * (half + 1)].bitcast(I32),
-                    in_=W_scales[4 * half : 4 * half + 4, 4 * q : 4 * q + 4, :].bitcast(I32),
+                nc.gpsimd.dma_start(
+                    out=planes[32 * q : 32 * q + 16, COLS * half : COLS * (half + 1)].bitcast(F32),
+                    in_=W_scales[4 * half : 4 * half + 4, 4 * q : 4 * q + 4, :].bitcast(F32),
                 )
         for g in range(GROUPS):
             src = W_words[g].rearrange("p n t -> p (n t)")

@@ -14,12 +14,9 @@ DIM = 4096
 COLS = 4608
 GROUPS = 8
 N_TILE = 512
-TILES = COLS // N_TILE
-TILES_A = 4
-COLS_A = TILES_A * N_TILE
-COLS_B = COLS - COLS_A
 HEADS_PER_TILE = 8
 TILES_PER_OUT = 3
+ROUNDS = ((0, 1, 2, 3), (4, 5, 6), (7, 8))
 
 FLOPS = 2 * TOKENS * DIM * COLS
 
@@ -27,16 +24,20 @@ FLOPS = 2 * TOKENS * DIM * COLS
 def tile_get_qkv_w_kernel(tc, x, W_words, W_scales, out_0, out_1, out_2):
     nc = tc.nc
     outs = [out_0, out_1, out_2]
-    with tc.tile_pool(name="keep", bufs=1) as keep, tc.psum_pool(name="psum", bufs=8) as psum, tc.manual_schedule():
+    with tc.tile_pool(name="keep", bufs=1) as keep, tc.tile_pool(name="turn", bufs=4) as turn, tc.psum_pool(
+        name="psum", bufs=8
+    ) as psum, tc.manual_schedule():
         planes = keep.tile([P, 2 * COLS], U8, align_bytes=64)
         x_sb = keep.tile([P, DIM], BF16, align_bytes=64)
         grouped = keep.tile([P, DIM], BF16, align_bytes=64)
         x_codes = keep.tile([P, GROUPS * TOKENS], U32, align_bytes=64)
         x_scales = keep.tile([P, GROUPS * TOKENS], U8, align_bytes=64)
         ident = keep.tile([P, P], F32)
-        w_a = [keep.tile([P, COLS_A], U32, align_bytes=64, name="w_a%d" % g) for g in range(GROUPS)]
-        w_b = [keep.tile([P, COLS_B], U32, align_bytes=64, name="w_b%d" % g) for g in range(GROUPS)]
-        stage = [keep.tile([P, TILES_PER_OUT * N_TILE], F32, name="stage%d" % o) for o in range(3)]
+        words = [
+            [keep.tile([P, N_TILE * len(tiles)], U32, align_bytes=64, name="w%d_%d" % (r, g)) for g in range(GROUPS)]
+            for r, tiles in enumerate(ROUNDS)
+        ]
+        rows = [keep.tile([P, N_TILE], F32, align_bytes=64, name="rows%d" % t) for t in range(9)]
 
         nc.vector.memset(planes[:].bitcast(I32), 0)
         make_identity(nc, ident[:])
@@ -49,12 +50,13 @@ def tile_get_qkv_w_kernel(tc, x, W_words, W_scales, out_0, out_1, out_2):
                     out=planes[32 * q : 32 * q + 16, COLS * half : COLS * (half + 1)].bitcast(F32),
                     in_=W_scales[4 * half : 4 * half + 4, 4 * q : 4 * q + 4, :].bitcast(F32),
                 )
-        for g in range(GROUPS):
-            src = W_words[g].rearrange("p n t -> p (n t)")
-            nc.sync.dma_start(out=w_a[g][:].bitcast(I32), in_=src[:, 0 : 4 * COLS_A].bitcast(I32))
-        for g in range(GROUPS):
-            src = W_words[g].rearrange("p n t -> p (n t)")
-            nc.sync.dma_start(out=w_b[g][:].bitcast(I32), in_=src[:, 4 * COLS_A : 4 * COLS].bitcast(I32))
+        for r, tiles in enumerate(ROUNDS):
+            for g in range(GROUPS):
+                src = W_words[g].rearrange("p n t -> p (n t)")
+                nc.sync.dma_start(
+                    out=words[r][g][:].bitcast(I32),
+                    in_=src[:, 4 * N_TILE * tiles[0] : 4 * N_TILE * (tiles[-1] + 1)].bitcast(I32),
+                )
 
         x_words = x_sb[:].bitcast(F32)
         grouped_words = grouped[:].bitcast(F32)
@@ -77,48 +79,44 @@ def tile_get_qkv_w_kernel(tc, x, W_words, W_scales, out_0, out_1, out_2):
                 in_=grouped[:, 2048 * hq : 2048 * (hq + 1)],
             )
 
-        acc = {}
-
-        def one_pass(g, t):
-            if t < TILES_A:
-                words = w_a[g][:, N_TILE * t : N_TILE * (t + 1)]
-            else:
-                words = w_b[g][:, N_TILE * (t - TILES_A) : N_TILE * (t - TILES_A + 1)]
-            k = 4 * (g % 4)
-            c0 = COLS * (g // 4) + N_TILE * t
-            nc.tensor.matmul_mx(
-                out=acc[t][:],
-                lhsT=x_codes[:, TOKENS * g : TOKENS * (g + 1)].bitcast(FP8X4),
-                lhsT_scale=x_scales[:, TOKENS * g : TOKENS * (g + 1)],
-                rhs=words.bitcast(FP8X4),
-                rhs_scale=planes[k:P, c0 : c0 + N_TILE],
-                start=(g == 0),
-                stop=(g == GROUPS - 1),
-            )
-
-        def leave(t):
-            o, part = divmod(t, TILES_PER_OUT)
-            dst = stage[o][:, N_TILE * part : N_TILE * (part + 1)]
-            if t % 2 == 0:
-                nc.scalar.copy(out=dst, in_=acc[t][:])
-            else:
-                nc.vector.tensor_copy(out=dst, in_=acc[t][:])
-
-        def store(t):
-            o, part = divmod(t, TILES_PER_OUT)
-            for b in range(2):
-                nc.sync.dma_start(
-                    out=outs[o][b, HEADS_PER_TILE * part : HEADS_PER_TILE * (part + 1), :, :].rearrange("h n d -> n h d"),
-                    in_=stage[o][b:P:2, N_TILE * part : N_TILE * (part + 1)].rearrange("p (h d) -> p h d", h=HEADS_PER_TILE),
-                )
-
-        for tiles in (list(range(0, TILES_A)), list(range(TILES_A, TILES))):
+        for r, tiles in enumerate(ROUNDS):
+            acc = {}
+            first = {}
             for t in tiles:
                 acc[t] = psum.tile([P, N_TILE], F32, tag="bank", name="acc%d" % t)
             for g in range(GROUPS):
-                for t in tiles:
-                    one_pass(g, t)
-                    if g == GROUPS - 1:
-                        leave(t)
-        for t in range(TILES):
-            store(t)
+                k = 4 * (g % 4)
+                for i, t in enumerate(tiles):
+                    c0 = COLS * (g // 4) + N_TILE * t
+                    nc.tensor.matmul_mx(
+                        out=acc[t][:],
+                        lhsT=x_codes[:, TOKENS * g : TOKENS * (g + 1)].bitcast(FP8X4),
+                        lhsT_scale=x_scales[:, TOKENS * g : TOKENS * (g + 1)],
+                        rhs=words[r][g][:, N_TILE * i : N_TILE * (i + 1)].bitcast(FP8X4),
+                        rhs_scale=planes[k:P, c0 : c0 + N_TILE],
+                        start=(g == 0),
+                        stop=(g == GROUPS - 1),
+                    )
+            for t in tiles:
+                first[t] = turn.tile([P, N_TILE], F32, align_bytes=64, tag="first", name="first%d" % t)
+                nc.vector.transpose(out=first[t][:], in_=acc[t][:])
+            for t in tiles:
+                sorted_t = turn.tile([P, N_TILE], F32, align_bytes=64, tag="sorted", name="sorted%d" % t)
+                by_b = first[t][:].rearrange("p (h m l b) -> p b l m h", h=8, m=8, l=4, b=2)
+                for b in range(2):
+                    half_cols = slice(256 * b, 256 * (b + 1))
+                    nc.scalar.copy(
+                        out=sorted_t[:, half_cols].rearrange("p (l m h) -> p l m h", l=4, m=8),
+                        in_=by_b[:, b],
+                    )
+                    nc.vector.transpose(out=rows[t][:, half_cols], in_=sorted_t[:, half_cols])
+
+        for t in range(9):
+            o, part = divmod(t, TILES_PER_OUT)
+            for b in range(2):
+                nc.sync.dma_start(
+                    out=outs[o][b, HEADS_PER_TILE * part : HEADS_PER_TILE * (part + 1), :, :].rearrange(
+                        "h (nh l) d -> nh h (l d)", l=4
+                    ),
+                    in_=rows[t][:, 256 * b : 256 * (b + 1)],
+                )

@@ -17,6 +17,8 @@ N_TILE = 512
 HEADS_PER_TILE = 8
 TILES_PER_OUT = 3
 ROUNDS = ((0, 1, 2, 3), (4, 5, 6), (7, 8))
+WHOLE = 5
+LATE_TILE = 8
 
 FLOPS = 2 * TOKENS * DIM * COLS
 
@@ -33,8 +35,9 @@ def tile_get_qkv_w_kernel(tc, x, W_words, W_scales, out_0, out_1, out_2):
         x_codes = keep.tile([P, GROUPS * TOKENS], U32, align_bytes=64)
         x_scales = keep.tile([P, GROUPS * TOKENS], U8, align_bytes=64)
         ident = keep.tile([P, P], F32)
-        words = [
-            [keep.tile([P, N_TILE * len(tiles)], U32, align_bytes=64, name="w%d_%d" % (r, g)) for g in range(GROUPS)]
+        whole = [keep.tile([P, COLS], U32, align_bytes=64, name="whole%d" % g) for g in range(WHOLE)]
+        rest = [
+            keep.tile([P, GROUPS - WHOLE, N_TILE * len(tiles)], U32, align_bytes=64, name="rest%d" % r)
             for r, tiles in enumerate(ROUNDS)
         ]
         rows = [keep.tile([P, N_TILE], F32, align_bytes=64, name="rows%d" % t) for t in range(9)]
@@ -50,13 +53,14 @@ def tile_get_qkv_w_kernel(tc, x, W_words, W_scales, out_0, out_1, out_2):
                     out=planes[32 * q : 32 * q + 16, COLS * half : COLS * (half + 1)].bitcast(F32),
                     in_=W_scales[4 * half : 4 * half + 4, 4 * q : 4 * q + 4, :].bitcast(F32),
                 )
+        for g in range(WHOLE):
+            nc.sync.dma_start(out=whole[g][:].bitcast(I32), in_=W_words[g].rearrange("p n t -> p (n t)").bitcast(I32))
         for r, tiles in enumerate(ROUNDS):
-            for g in range(GROUPS):
-                src = W_words[g].rearrange("p n t -> p (n t)")
-                nc.sync.dma_start(
-                    out=words[r][g][:].bitcast(I32),
-                    in_=src[:, 4 * N_TILE * tiles[0] : 4 * N_TILE * (tiles[-1] + 1)].bitcast(I32),
-                )
+            src = W_words[WHOLE:GROUPS].rearrange("g p n t -> p g (n t)")
+            nc.sync.dma_start(
+                out=rest[r][:].bitcast(I32),
+                in_=src[:, :, 4 * N_TILE * tiles[0] : 4 * N_TILE * (tiles[-1] + 1)].bitcast(I32),
+            )
 
         x_words = x_sb[:].bitcast(F32)
         grouped_words = grouped[:].bitcast(F32)
@@ -79,24 +83,36 @@ def tile_get_qkv_w_kernel(tc, x, W_words, W_scales, out_0, out_1, out_2):
                 in_=grouped[:, 2048 * hq : 2048 * (hq + 1)],
             )
 
+        acc = {}
+
+        def one_pass(g, t, w_cols):
+            k = 4 * (g % 4)
+            c0 = COLS * (g // 4) + N_TILE * t
+            nc.tensor.matmul_mx(
+                out=acc[t][:],
+                lhsT=x_codes[:, TOKENS * g : TOKENS * (g + 1)].bitcast(FP8X4),
+                lhsT_scale=x_scales[:, TOKENS * g : TOKENS * (g + 1)],
+                rhs=w_cols.bitcast(FP8X4),
+                rhs_scale=planes[k:P, c0 : c0 + N_TILE],
+                start=(g == 0),
+                stop=(g == GROUPS - 1),
+            )
+
+        for t in range(LATE_TILE):
+            acc[t] = psum.tile([P, N_TILE], F32, tag="bank", name="acc%d" % t)
+        for g in range(WHOLE):
+            for t in range(LATE_TILE):
+                one_pass(g, t, whole[g][:, N_TILE * t : N_TILE * (t + 1)])
+
         for r, tiles in enumerate(ROUNDS):
-            acc = {}
             first = {}
-            for t in tiles:
-                acc[t] = psum.tile([P, N_TILE], F32, tag="bank", name="acc%d" % t)
-            for g in range(GROUPS):
-                k = 4 * (g % 4)
+            if LATE_TILE in tiles:
+                acc[LATE_TILE] = psum.tile([P, N_TILE], F32, tag="bank", name="acc%d" % LATE_TILE)
+                for g in range(WHOLE):
+                    one_pass(g, LATE_TILE, whole[g][:, N_TILE * LATE_TILE : N_TILE * (LATE_TILE + 1)])
+            for g in range(WHOLE, GROUPS):
                 for i, t in enumerate(tiles):
-                    c0 = COLS * (g // 4) + N_TILE * t
-                    nc.tensor.matmul_mx(
-                        out=acc[t][:],
-                        lhsT=x_codes[:, TOKENS * g : TOKENS * (g + 1)].bitcast(FP8X4),
-                        lhsT_scale=x_scales[:, TOKENS * g : TOKENS * (g + 1)],
-                        rhs=words[r][g][:, N_TILE * i : N_TILE * (i + 1)].bitcast(FP8X4),
-                        rhs_scale=planes[k:P, c0 : c0 + N_TILE],
-                        start=(g == 0),
-                        stop=(g == GROUPS - 1),
-                    )
+                    one_pass(g, t, rest[r][:, g - WHOLE, N_TILE * i : N_TILE * (i + 1)])
             for t in tiles:
                 first[t] = turn.tile([P, N_TILE], F32, align_bytes=64, tag="first", name="first%d" % t)
                 nc.vector.transpose(out=first[t][:], in_=acc[t][:])

@@ -17,8 +17,6 @@ N_TILE = 512
 HEADS_PER_TILE = 8
 TILES_PER_OUT = 3
 ROUNDS = ((0, 1, 2, 3), (4, 5, 6), (7, 8))
-WHOLE = 5
-LATE_TILE = 8
 
 FLOPS = 2 * TOKENS * DIM * COLS
 
@@ -35,9 +33,8 @@ def tile_get_qkv_w_kernel(tc, x, W_words, W_scales, out_0, out_1, out_2):
         x_codes = keep.tile([P, GROUPS * TOKENS], U32, align_bytes=64)
         x_scales = keep.tile([P, GROUPS * TOKENS], U8, align_bytes=64)
         ident = keep.tile([P, P], F32)
-        whole = [keep.tile([P, COLS], U32, align_bytes=64, name="whole%d" % g) for g in range(WHOLE)]
-        rest = [
-            keep.tile([P, GROUPS - WHOLE, N_TILE * len(tiles)], U32, align_bytes=64, name="rest%d" % r)
+        words = [
+            [keep.tile([P, N_TILE * len(tiles)], U32, align_bytes=64, name="w%d_%d" % (r, g)) for g in range(GROUPS)]
             for r, tiles in enumerate(ROUNDS)
         ]
         rows = [keep.tile([P, N_TILE], F32, align_bytes=64, name="rows%d" % t) for t in range(9)]
@@ -53,14 +50,15 @@ def tile_get_qkv_w_kernel(tc, x, W_words, W_scales, out_0, out_1, out_2):
                     out=planes[32 * q : 32 * q + 16, COLS * half : COLS * (half + 1)].bitcast(F32),
                     in_=W_scales[4 * half : 4 * half + 4, 4 * q : 4 * q + 4, :].bitcast(F32),
                 )
-        for g in range(WHOLE):
-            nc.sync.dma_start(out=whole[g][:].bitcast(I32), in_=W_words[g].rearrange("p n t -> p (n t)").bitcast(I32))
         for r, tiles in enumerate(ROUNDS):
-            src = W_words[WHOLE:GROUPS].rearrange("g p n t -> p g (n t)")
-            nc.sync.dma_start(
-                out=rest[r][:].bitcast(I32),
-                in_=src[:, :, 4 * N_TILE * tiles[0] : 4 * N_TILE * (tiles[-1] + 1)].bitcast(I32),
-            )
+            for g in range(GROUPS):
+                src = W_words[g].rearrange("p n t -> p (n t)")
+                very_last = r == len(ROUNDS) - 1 and g == GROUPS - 1
+                for cut in [(t,) for t in tiles] if very_last else [tiles]:
+                    nc.sync.dma_start(
+                        out=words[r][g][:, N_TILE * (cut[0] - tiles[0]) : N_TILE * (cut[-1] + 1 - tiles[0])].bitcast(I32),
+                        in_=src[:, 4 * N_TILE * cut[0] : 4 * N_TILE * (cut[-1] + 1)].bitcast(I32),
+                    )
 
         x_words = x_sb[:].bitcast(F32)
         grouped_words = grouped[:].bitcast(F32)
@@ -83,53 +81,44 @@ def tile_get_qkv_w_kernel(tc, x, W_words, W_scales, out_0, out_1, out_2):
                 in_=grouped[:, 2048 * hq : 2048 * (hq + 1)],
             )
 
-        acc = {}
-
-        def one_pass(g, t, w_cols):
-            k = 4 * (g % 4)
-            c0 = COLS * (g // 4) + N_TILE * t
-            nc.tensor.matmul_mx(
-                out=acc[t][:],
-                lhsT=x_codes[:, TOKENS * g : TOKENS * (g + 1)].bitcast(FP8X4),
-                lhsT_scale=x_scales[:, TOKENS * g : TOKENS * (g + 1)],
-                rhs=w_cols.bitcast(FP8X4),
-                rhs_scale=planes[k:P, c0 : c0 + N_TILE],
-                start=(g == 0),
-                stop=(g == GROUPS - 1),
-            )
-
-        for t in range(LATE_TILE):
-            acc[t] = psum.tile([P, N_TILE], F32, tag="bank", name="acc%d" % t)
-        for g in range(WHOLE):
-            for t in range(LATE_TILE):
-                one_pass(g, t, whole[g][:, N_TILE * t : N_TILE * (t + 1)])
-
         for r, tiles in enumerate(ROUNDS):
+            acc = {}
             first = {}
-            if LATE_TILE in tiles:
-                acc[LATE_TILE] = psum.tile([P, N_TILE], F32, tag="bank", name="acc%d" % LATE_TILE)
-                for g in range(WHOLE):
-                    one_pass(g, LATE_TILE, whole[g][:, N_TILE * LATE_TILE : N_TILE * (LATE_TILE + 1)])
-            for g in range(WHOLE, GROUPS):
+            resorted = {}
+            for t in tiles:
+                acc[t] = psum.tile([P, N_TILE], F32, tag="bank", name="acc%d" % t)
+            for g in range(GROUPS):
+                k = 4 * (g % 4)
                 for i, t in enumerate(tiles):
-                    one_pass(g, t, rest[r][:, g - WHOLE, N_TILE * i : N_TILE * (i + 1)])
+                    c0 = COLS * (g // 4) + N_TILE * t
+                    nc.tensor.matmul_mx(
+                        out=acc[t][:],
+                        lhsT=x_codes[:, TOKENS * g : TOKENS * (g + 1)].bitcast(FP8X4),
+                        lhsT_scale=x_scales[:, TOKENS * g : TOKENS * (g + 1)],
+                        rhs=words[r][g][:, N_TILE * i : N_TILE * (i + 1)].bitcast(FP8X4),
+                        rhs_scale=planes[k:P, c0 : c0 + N_TILE],
+                        start=(g == 0),
+                        stop=(g == GROUPS - 1),
+                    )
             for t in tiles:
                 first[t] = turn.tile([P, N_TILE], F32, align_bytes=64, tag="first", name="first%d" % t)
                 nc.vector.transpose(out=first[t][:], in_=acc[t][:])
-            for t in tiles:
-                sorted_t = turn.tile([P, N_TILE], F32, align_bytes=64, tag="sorted", name="sorted%d" % t)
+                resorted[t] = turn.tile([P, N_TILE], F32, align_bytes=64, tag="sorted", name="sorted%d" % t)
                 by_b = first[t][:].rearrange("p (h m l b) -> p b l m h", h=8, m=8, l=4, b=2)
-                for b in range(2):
+                for b in (1, 0):
+                    dst = resorted[t][:, 256 * b : 256 * (b + 1)].rearrange("p (l m h) -> p l m h", l=4, m=8)
+                    if b == 1:
+                        nc.vector.tensor_copy(out=dst, in_=by_b[:, b])
+                    else:
+                        nc.scalar.copy(out=dst, in_=by_b[:, b])
+            for t in tiles:
+                for b in (1, 0):
                     half_cols = slice(256 * b, 256 * (b + 1))
-                    nc.scalar.copy(
-                        out=sorted_t[:, half_cols].rearrange("p (l m h) -> p l m h", l=4, m=8),
-                        in_=by_b[:, b],
-                    )
-                    nc.vector.transpose(out=rows[t][:, half_cols], in_=sorted_t[:, half_cols])
+                    nc.vector.transpose(out=rows[t][:, half_cols], in_=resorted[t][:, half_cols])
 
         for t in range(9):
             o, part = divmod(t, TILES_PER_OUT)
-            for b in range(2):
+            for b in (1, 0):
                 nc.sync.dma_start(
                     out=outs[o][b, HEADS_PER_TILE * part : HEADS_PER_TILE * (part + 1), :, :].rearrange(
                         "h (nh l) d -> nh h (l d)", l=4

@@ -100,6 +100,13 @@ def tile_get_qkv_w_kernel(tc, x, W_words, W_scales, out_0, out_1, out_2):
                         start=(g == 0),
                         stop=(g == GROUPS - 1),
                     )
+            if r == len(ROUNDS) - 1:
+                for i, t in enumerate(tiles):
+                    if i % 2 == 0:
+                        nc.scalar.copy(out=rows[t][:], in_=acc[t][:])
+                    else:
+                        nc.vector.tensor_copy(out=rows[t][:], in_=acc[t][:])
+                continue
             for t in tiles:
                 first[t] = turn.tile([P, N_TILE], F32, align_bytes=64, tag="first", name="first%d" % t)
                 nc.vector.transpose(out=first[t][:], in_=acc[t][:])
@@ -118,6 +125,13 @@ def tile_get_qkv_w_kernel(tc, x, W_words, W_scales, out_0, out_1, out_2):
 
         for t in range(9):
             o, part = divmod(t, TILES_PER_OUT)
+            if t in ROUNDS[-1]:
+                for b in (1, 0):
+                    nc.sync.dma_start(
+                        out=outs[o][b, HEADS_PER_TILE * part : HEADS_PER_TILE * (part + 1), :, :].rearrange("h n d -> n h d"),
+                        in_=rows[t][b:P:2, :].rearrange("p (h d) -> p h d", h=HEADS_PER_TILE),
+                    )
+                continue
             for b in (1, 0):
                 nc.sync.dma_start(
                     out=outs[o][b, HEADS_PER_TILE * part : HEADS_PER_TILE * (part + 1), :, :].rearrange(

@@ -17,6 +17,7 @@ N_TILE = 512
 HEADS_PER_TILE = 8
 TILES_PER_OUT = 3
 ROUNDS = ((0, 1, 2, 3), (4, 5, 6), (7, 8))
+WHOLE = 4
 
 FLOPS = 2 * TOKENS * DIM * COLS
 
@@ -33,8 +34,12 @@ def tile_get_qkv_w_kernel(tc, x, W_words, W_scales, out_0, out_1, out_2):
         x_codes = keep.tile([P, GROUPS * TOKENS], U32, align_bytes=64)
         x_scales = keep.tile([P, GROUPS * TOKENS], U8, align_bytes=64)
         ident = keep.tile([P, P], F32)
+        whole = [keep.tile([P, COLS], U32, align_bytes=64, name="whole%d" % g) for g in range(WHOLE)]
         words = [
-            [keep.tile([P, N_TILE * len(tiles)], U32, align_bytes=64, name="w%d_%d" % (r, g)) for g in range(GROUPS)]
+            [
+                keep.tile([P, N_TILE * len(tiles)], U32, align_bytes=64, name="w%d_%d" % (r, g))
+                for g in range(WHOLE, GROUPS)
+            ]
             for r, tiles in enumerate(ROUNDS)
         ]
         rows = [keep.tile([P, N_TILE], F32, align_bytes=64, name="rows%d" % t) for t in range(9)]
@@ -50,13 +55,15 @@ def tile_get_qkv_w_kernel(tc, x, W_words, W_scales, out_0, out_1, out_2):
                     out=planes[32 * q : 32 * q + 16, COLS * half : COLS * (half + 1)].bitcast(F32),
                     in_=W_scales[4 * half : 4 * half + 4, 4 * q : 4 * q + 4, :].bitcast(F32),
                 )
+        for g in range(WHOLE):
+            nc.sync.dma_start(out=whole[g][:].bitcast(I32), in_=W_words[g].rearrange("p n t -> p (n t)").bitcast(I32))
         for r, tiles in enumerate(ROUNDS):
-            for g in range(GROUPS):
+            for g in range(WHOLE, GROUPS):
                 src = W_words[g].rearrange("p n t -> p (n t)")
                 very_last = r == len(ROUNDS) - 1 and g == GROUPS - 1
                 for cut in [(t,) for t in tiles] if very_last else [tiles]:
                     nc.sync.dma_start(
-                        out=words[r][g][:, N_TILE * (cut[0] - tiles[0]) : N_TILE * (cut[-1] + 1 - tiles[0])].bitcast(I32),
+                        out=words[r][g - WHOLE][:, N_TILE * (cut[0] - tiles[0]) : N_TILE * (cut[-1] + 1 - tiles[0])].bitcast(I32),
                         in_=src[:, 4 * N_TILE * cut[0] : 4 * N_TILE * (cut[-1] + 1)].bitcast(I32),
                     )
 
@@ -95,7 +102,11 @@ def tile_get_qkv_w_kernel(tc, x, W_words, W_scales, out_0, out_1, out_2):
                         out=acc[t][:],
                         lhsT=x_codes[:, TOKENS * g : TOKENS * (g + 1)].bitcast(FP8X4),
                         lhsT_scale=x_scales[:, TOKENS * g : TOKENS * (g + 1)],
-                        rhs=words[r][g][:, N_TILE * i : N_TILE * (i + 1)].bitcast(FP8X4),
+                        rhs=(
+                            whole[g][:, N_TILE * t : N_TILE * (t + 1)]
+                            if g < WHOLE
+                            else words[r][g - WHOLE][:, N_TILE * i : N_TILE * (i + 1)]
+                        ).bitcast(FP8X4),
                         rhs_scale=planes[k:P, c0 : c0 + N_TILE],
                         start=(g == 0),
                         stop=(g == GROUPS - 1),

@@ -44,7 +44,8 @@ def tile_get_qkv_w_kernel(tc, x, W_words, W_scales, out_0, out_1, out_2):
         ]
         rows = [keep.tile([P, N_TILE], F32, align_bytes=64, name="rows%d" % t) for t in range(9)]
 
-        nc.vector.memset(planes[:].bitcast(I32), 0)
+        for half in range(2):
+            nc.vector.memset(planes[:, COLS * half : COLS * (half + 1)].bitcast(I32), 0)
         make_identity(nc, ident[:])
 
         for b in range(2):
@@ -55,6 +56,7 @@ def tile_get_qkv_w_kernel(tc, x, W_words, W_scales, out_0, out_1, out_2):
                     out=planes[32 * q : 32 * q + 16, COLS * half : COLS * (half + 1)].bitcast(F32),
                     in_=W_scales[4 * half : 4 * half + 4, 4 * q : 4 * q + 4, :].bitcast(F32),
                 )
+            nc.gpsimd.memset(whole[half + 1][:, 0:16].bitcast(F32), 0.0)
         for g in range(WHOLE):
             nc.sync.dma_start(out=whole[g][:].bitcast(I32), in_=W_words[g].rearrange("p n t -> p (n t)").bitcast(I32))
         for r, tiles in enumerate(ROUNDS):

@@ -34,6 +34,7 @@ def tile_get_qkv_w_kernel(tc, x, W_words, W_scales, out_0, out_1, out_2):
         x_codes = keep.tile([P, GROUPS * TOKENS], U32, align_bytes=64)
         x_scales = keep.tile([P, GROUPS * TOKENS], U8, align_bytes=64)
         ident = keep.tile([P, P], F32)
+        perm = keep.tile([P, P], F32)
         whole = [keep.tile([P, COLS], U32, align_bytes=64, name="whole%d" % g) for g in range(WHOLE)]
         words = [
             [
@@ -47,9 +48,11 @@ def tile_get_qkv_w_kernel(tc, x, W_words, W_scales, out_0, out_1, out_2):
         for half in range(2):
             nc.vector.memset(planes[:, COLS * half : COLS * (half + 1)].bitcast(I32), 0)
         make_identity(nc, ident[:])
+        nc.vector.tensor_copy(
+            out=perm[:].rearrange("p (n b) -> p b n", b=2), in_=ident[:].rearrange("p (b n) -> p b n", b=2)
+        )
 
-        for b in range(2):
-            nc.sync.dma_start(out=x_sb[b:P:2, :], in_=x[b])
+        nc.sync.dma_start(out=x_sb[:], in_=x.rearrange("b n d -> (b n) d"))
         for half in range(2):
             for q in range(4):
                 nc.gpsimd.dma_start(
@@ -76,7 +79,7 @@ def tile_get_qkv_w_kernel(tc, x, W_words, W_scales, out_0, out_1, out_2):
             for gg in range(2):
                 for u in range(2):
                     g = 2 * a + gg
-                    nc.tensor.transpose(xt[:, 2 * gg + u, :], x_words[:, 256 * g + u : 256 * (g + 1) : 2], ident[:])
+                    nc.tensor.transpose(xt[:, 2 * gg + u, :], x_words[:, 256 * g + u : 256 * (g + 1) : 2], perm[:])
             dst = grouped_words[:, 512 * a : 512 * (a + 1)].rearrange("p (g t u) -> p g t u", g=2, u=2)
             view = xt[:].rearrange("p (g u) t -> p g t u", u=2)
             if a % 2 == 0:

@@ -26,10 +26,12 @@ def tile_get_qkv_w_kernel(tc, x, W_words, W_scales, out_0, out_1, out_2):
     nc = tc.nc
     outs = [out_0, out_1, out_2]
     with tc.tile_pool(name="keep", bufs=1) as keep, tc.tile_pool(name="turn", bufs=4) as turn, tc.psum_pool(
-        name="psum", bufs=8
-    ) as psum, tc.manual_schedule():
+        name="psum", bufs=6
+    ) as psum, tc.psum_pool(name="psum_x", bufs=2) as psum_x, tc.manual_schedule():
         planes = keep.tile([P, 2 * COLS], U8, align_bytes=64)
-        x_sb = keep.tile([P, DIM], BF16, align_bytes=64)
+        x_sb = keep.tile([P, DIM // 2], BF16, align_bytes=64)
+        x_side = keep.tile([P, DIM], BF16, align_bytes=64)
+        perm_side = keep.tile([P, P], F32)
         grouped = keep.tile([P, DIM], BF16, align_bytes=64)
         x_codes = keep.tile([P, GROUPS * TOKENS], U32, align_bytes=64)
         x_scales = keep.tile([P, GROUPS * TOKENS], U8, align_bytes=64)
@@ -45,21 +47,37 @@ def tile_get_qkv_w_kernel(tc, x, W_words, W_scales, out_0, out_1, out_2):
         ]
         rows = [keep.tile([P, N_TILE], F32, align_bytes=64, name="rows%d" % t) for t in range(9)]
 
-        for half in range(2):
-            nc.vector.memset(planes[:, COLS * half : COLS * (half + 1)].bitcast(I32), 0)
+        nc.vector.memset(planes[:, 0:COLS].bitcast(I32), 0)
+        nc.vector.memset(x_side[:].bitcast(F32), 0.0)
+        nc.vector.memset(planes[:, COLS : 2 * COLS].bitcast(I32), 0)
         make_identity(nc, ident[:])
         nc.vector.tensor_copy(
             out=perm[:].rearrange("p (n b) -> p b n", b=2), in_=ident[:].rearrange("p (b n) -> p b n", b=2)
         )
 
-        nc.sync.dma_start(out=x_sb[:], in_=x.rearrange("b n d -> (b n) d"))
+        for z in range(2):
+            nc.vector.tensor_copy(
+                out=perm_side[:, 64 * (1 - z) : 64 * (2 - z)].rearrange("p (i q r) -> p i q r", i=4, q=4),
+                in_=ident[:].rearrange("p (q z i r) -> p z i q r", q=4, z=2, i=4)[:, z],
+            )
+
+        nc.sync.dma_start(out=x_sb[:], in_=x.rearrange("b n d -> (b n) d")[:, 0 : DIM // 2])
         for half in range(2):
-            for q in range(4):
+            for j, q in enumerate((0, 2, 1, 3)):
                 nc.gpsimd.dma_start(
                     out=planes[32 * q : 32 * q + 16, COLS * half : COLS * (half + 1)].bitcast(F32),
                     in_=W_scales[4 * half : 4 * half + 4, 4 * q : 4 * q + 4, :].bitcast(F32),
                 )
-            nc.gpsimd.memset(whole[half + 1][:, 0:16].bitcast(F32), 0.0)
+                nc.gpsimd.dma_start(
+                    out=x_side[32 * q + 16 : 32 * q + 32, (DIM // 2) * half : (DIM // 2) * (half + 1)],
+                    in_=x[half].rearrange("(i q r) d -> q i r d", i=4, q=4, r=4)[q, :, :, DIM // 2 : DIM],
+                )
+                if half == 0 and j == 1:
+                    nc.gpsimd.memset(whole[1][:, 0:16].bitcast(F32), 0.0)
+                if half == 0 and j == 3:
+                    nc.gpsimd.memset(whole[2][:, 0:16].bitcast(F32), 0.0)
+                if half == 1 and j == 3:
+                    nc.gpsimd.memset(words[0][0][:, 0:16].bitcast(F32), 0.0)
         for g in range(WHOLE):
             nc.sync.dma_start(out=whole[g][:].bitcast(I32), in_=W_words[g].rearrange("p n t -> p (n t)").bitcast(I32))
         for r, tiles in enumerate(ROUNDS):
@@ -74,8 +92,8 @@ def tile_get_qkv_w_kernel(tc, x, W_words, W_scales, out_0, out_1, out_2):
 
         x_words = x_sb[:].bitcast(F32)
         grouped_words = grouped[:].bitcast(F32)
-        for a in range(4):
-            xt = psum.tile([P, 4, TOKENS], F32, tag="bank", name="xt%d" % a)
+        for a in range(2):
+            xt = psum_x.tile([P, 4, TOKENS], F32, tag="bank_x", name="xt%d" % a)
             for gg in range(2):
                 for u in range(2):
                     g = 2 * a + gg
@@ -86,12 +104,31 @@ def tile_get_qkv_w_kernel(tc, x, W_words, W_scales, out_0, out_1, out_2):
                 nc.vector.tensor_copy(out=dst, in_=view)
             else:
                 nc.scalar.copy(out=dst, in_=view)
-        for hq in range(2):
+
+        def quantize_half(hq):
             nc.vector.quantize_mx(
                 out=x_codes[:, 512 * hq : 512 * (hq + 1)].bitcast(FP8X4),
                 scales=x_scales[:, 512 * hq : 512 * (hq + 1)],
                 in_=grouped[:, 2048 * hq : 2048 * (hq + 1)],
             )
+
+        def second_half_of_x():
+            side_words = x_side[:].bitcast(F32)
+            for g in range(4, GROUPS):
+                xs = psum_x.tile([P, 4, TOKENS], F32, tag="bank_x", name="xs%d" % g)
+                for b in range(2):
+                    for u in range(2):
+                        c0 = 1024 * b + 256 * (g - 4)
+                        nc.tensor.transpose(xs[:, 2 * b + u, :], side_words[:, c0 + u : c0 + 256 : 2], perm_side[:])
+                dst = grouped_words[:, 256 * g : 256 * (g + 1)].rearrange("p (n v) -> p n v", v=4)
+                view = xs[:, :, 0:64].rearrange("p v n -> p n v")
+                if g % 2 == 0:
+                    nc.vector.tensor_copy(out=dst, in_=view)
+                else:
+                    nc.scalar.copy(out=dst, in_=view)
+            quantize_half(1)
+
+        quantize_half(0)
 
         for r, tiles in enumerate(ROUNDS):
             acc = {}
@@ -100,6 +137,8 @@ def tile_get_qkv_w_kernel(tc, x, W_words, W_scales, out_0, out_1, out_2):
             for t in tiles:
                 acc[t] = psum.tile([P, N_TILE], F32, tag="bank", name="acc%d" % t)
             for g in range(GROUPS):
+                if r == 0 and g == 4:
+                    second_half_of_x()
                 k = 4 * (g % 4)
                 for i, t in enumerate(tiles):
                     c0 = COLS * (g // 4) + N_TILE * t

@@ -17,6 +17,7 @@ N_TILE = 512
 HEADS_PER_TILE = 8
 TILES_PER_OUT = 3
 ROUNDS = ((0, 1, 2, 3), (4, 5, 6), (7, 8))
+SHORT = 8
 WHOLE = 4
 
 FLOPS = 2 * TOKENS * DIM * COLS
@@ -155,32 +156,30 @@ def tile_get_qkv_w_kernel(tc, x, W_words, W_scales, out_0, out_1, out_2):
                         start=(g == 0),
                         stop=(g == GROUPS - 1),
                     )
-            if r == len(ROUNDS) - 1:
-                for i, t in enumerate(tiles):
-                    if i % 2 == 0:
-                        nc.scalar.copy(out=rows[t][:], in_=acc[t][:])
-                    else:
-                        nc.vector.tensor_copy(out=rows[t][:], in_=acc[t][:])
-                continue
             for t in tiles:
+                if t == SHORT:
+                    nc.scalar.copy(out=rows[t][:], in_=acc[t][:])
+                    continue
                 first[t] = turn.tile([P, N_TILE], F32, align_bytes=64, tag="first", name="first%d" % t)
                 nc.vector.transpose(out=first[t][:], in_=acc[t][:])
                 resorted[t] = turn.tile([P, N_TILE], F32, align_bytes=64, tag="sorted", name="sorted%d" % t)
                 by_b = first[t][:].rearrange("p (h m l b) -> p b l m h", h=8, m=8, l=4, b=2)
                 for b in (1, 0):
                     dst = resorted[t][:, 256 * b : 256 * (b + 1)].rearrange("p (l m h) -> p l m h", l=4, m=8)
-                    if b == 1:
+                    if b == 1 or r == len(ROUNDS) - 1:
                         nc.vector.tensor_copy(out=dst, in_=by_b[:, b])
                     else:
                         nc.scalar.copy(out=dst, in_=by_b[:, b])
             for t in tiles:
+                if t == SHORT:
+                    continue
                 for b in (1, 0):
                     half_cols = slice(256 * b, 256 * (b + 1))
                     nc.vector.transpose(out=rows[t][:, half_cols], in_=resorted[t][:, half_cols])
 
-        for t in range(9):
+        for t in (0, 1, 2, 3, 4, 5, 6, 8, 7):
             o, part = divmod(t, TILES_PER_OUT)
-            if t in ROUNDS[-1]:
+            if t == SHORT:
                 for b in (1, 0):
                     nc.sync.dma_start(
                         out=outs[o][b, HEADS_PER_TILE * part : HEADS_PER_TILE * (part + 1), :, :].rearrange("h n d -> n h d"),

import concourse.mybir as mybir
from concourse.masks import make_identity

F32 = mybir.dt.float32
BF16 = mybir.dt.bfloat16
U8 = mybir.dt.uint8
U32 = mybir.dt.uint32
I32 = mybir.dt.int32
FP8X4 = mybir.dt.float8_e4m3fn_x4

P = 128
TOKENS = 128
DIM = 4096
COLS = 4608
GROUPS = 8
N_TILE = 512
HEADS_PER_TILE = 8
TILES_PER_OUT = 3
ROUNDS = ((0, 1, 2, 3), (4, 5, 6), (7, 8))
SHORT = 8
WHOLE = 4

FLOPS = 2 * TOKENS * DIM * COLS


def tile_get_qkv_w_kernel(tc, x, W_words, W_scales, out_0, out_1, out_2):
    nc = tc.nc
    outs = [out_0, out_1, out_2]
    with tc.tile_pool(name="keep", bufs=1) as keep, tc.tile_pool(name="turn", bufs=4) as turn, tc.psum_pool(
        name="psum", bufs=6
    ) as psum, tc.psum_pool(name="psum_x", bufs=2) as psum_x, tc.manual_schedule():
        planes = keep.tile([P, 2 * COLS], U8, align_bytes=64)
        x_sb = keep.tile([P, DIM // 2], BF16, align_bytes=64)
        x_side = keep.tile([P, DIM], BF16, align_bytes=64)
        perm_side = keep.tile([P, P], F32)
        grouped = keep.tile([P, DIM], BF16, align_bytes=64)
        x_codes = keep.tile([P, GROUPS * TOKENS], U32, align_bytes=64)
        x_scales = keep.tile([P, GROUPS * TOKENS], U8, align_bytes=64)
        ident = keep.tile([P, P], F32)
        perm = keep.tile([P, P], F32)
        whole = [keep.tile([P, COLS], U32, align_bytes=64, name="whole%d" % g) for g in range(WHOLE)]
        words = [
            [
                keep.tile([P, N_TILE * len(tiles)], U32, align_bytes=64, name="w%d_%d" % (r, g))
                for g in range(WHOLE, GROUPS)
            ]
            for r, tiles in enumerate(ROUNDS)
        ]
        rows = [keep.tile([P, N_TILE], F32, align_bytes=64, name="rows%d" % t) for t in range(9)]

        nc.vector.memset(planes[:, 0:COLS].bitcast(I32), 0)
        nc.vector.memset(x_side[:].bitcast(F32), 0.0)
        nc.vector.memset(planes[:, COLS : 2 * COLS].bitcast(I32), 0)
        make_identity(nc, ident[:])
        nc.vector.tensor_copy(
            out=perm[:].rearrange("p (n b) -> p b n", b=2), in_=ident[:].rearrange("p (b n) -> p b n", b=2)
        )

        for z in range(2):
            nc.vector.tensor_copy(
                out=perm_side[:, 64 * (1 - z) : 64 * (2 - z)].rearrange("p (i q r) -> p i q r", i=4, q=4),
                in_=ident[:].rearrange("p (q z i r) -> p z i q r", q=4, z=2, i=4)[:, z],
            )

        nc.sync.dma_start(out=x_sb[:], in_=x.rearrange("b n d -> (b n) d")[:, 0 : DIM // 2])
        for half in range(2):
            for j, q in enumerate((0, 2, 1, 3)):
                nc.gpsimd.dma_start(
                    out=planes[32 * q : 32 * q + 16, COLS * half : COLS * (half + 1)].bitcast(F32),
                    in_=W_scales[4 * half : 4 * half + 4, 4 * q : 4 * q + 4, :].bitcast(F32),
                )
                nc.gpsimd.dma_start(
                    out=x_side[32 * q + 16 : 32 * q + 32, (DIM // 2) * half : (DIM // 2) * (half + 1)],
                    in_=x[half].rearrange("(i q r) d -> q i r d", i=4, q=4, r=4)[q, :, :, DIM // 2 : DIM],
                )
                if half == 0 and j == 1:
                    nc.gpsimd.memset(whole[1][:, 0:16].bitcast(F32), 0.0)
                if half == 0 and j == 3:
                    nc.gpsimd.memset(whole[2][:, 0:16].bitcast(F32), 0.0)
                if half == 1 and j == 3:
                    nc.gpsimd.memset(words[0][0][:, 0:16].bitcast(F32), 0.0)
        for g in range(WHOLE):
            nc.sync.dma_start(out=whole[g][:].bitcast(I32), in_=W_words[g].rearrange("p n t -> p (n t)").bitcast(I32))
        for r, tiles in enumerate(ROUNDS):
            for g in range(WHOLE, GROUPS):
                src = W_words[g].rearrange("p n t -> p (n t)")
                very_last = r == len(ROUNDS) - 1 and g == GROUPS - 1
                for cut in [(t,) for t in tiles] if very_last else [tiles]:
                    nc.sync.dma_start(
                        out=words[r][g - WHOLE][:, N_TILE * (cut[0] - tiles[0]) : N_TILE * (cut[-1] + 1 - tiles[0])].bitcast(I32),
                        in_=src[:, 4 * N_TILE * cut[0] : 4 * N_TILE * (cut[-1] + 1)].bitcast(I32),
                    )

        x_words = x_sb[:].bitcast(F32)
        grouped_words = grouped[:].bitcast(F32)
        for a in range(2):
            xt = psum_x.tile([P, 4, TOKENS], F32, tag="bank_x", name="xt%d" % a)
            for gg in range(2):
                for u in range(2):
                    g = 2 * a + gg
                    nc.tensor.transpose(xt[:, 2 * gg + u, :], x_words[:, 256 * g + u : 256 * (g + 1) : 2], perm[:])
            dst = grouped_words[:, 512 * a : 512 * (a + 1)].rearrange("p (g t u) -> p g t u", g=2, u=2)
            view = xt[:].rearrange("p (g u) t -> p g t u", u=2)
            if a % 2 == 0:
                nc.vector.tensor_copy(out=dst, in_=view)
            else:
                nc.scalar.copy(out=dst, in_=view)

        def quantize_half(hq):
            nc.vector.quantize_mx(
                out=x_codes[:, 512 * hq : 512 * (hq + 1)].bitcast(FP8X4),
                scales=x_scales[:, 512 * hq : 512 * (hq + 1)],
                in_=grouped[:, 2048 * hq : 2048 * (hq + 1)],
            )

        def second_half_of_x():
            side_words = x_side[:].bitcast(F32)
            for g in range(4, GROUPS):
                xs = psum_x.tile([P, 4, TOKENS], F32, tag="bank_x", name="xs%d" % g)
                for b in range(2):
                    for u in range(2):
                        c0 = 1024 * b + 256 * (g - 4)
                        nc.tensor.transpose(xs[:, 2 * b + u, :], side_words[:, c0 + u : c0 + 256 : 2], perm_side[:])
                dst = grouped_words[:, 256 * g : 256 * (g + 1)].rearrange("p (n v) -> p n v", v=4)
                view = xs[:, :, 0:64].rearrange("p v n -> p n v")
                if g % 2 == 0:
                    nc.vector.tensor_copy(out=dst, in_=view)
                else:
                    nc.scalar.copy(out=dst, in_=view)
            quantize_half(1)

        quantize_half(0)

        for r, tiles in enumerate(ROUNDS):
            acc = {}
            first = {}
            resorted = {}
            for t in tiles:
                acc[t] = psum.tile([P, N_TILE], F32, tag="bank", name="acc%d" % t)
            for g in range(GROUPS):
                if r == 0 and g == 4:
                    second_half_of_x()
                k = 4 * (g % 4)
                for i, t in enumerate(tiles):
                    c0 = COLS * (g // 4) + N_TILE * t
                    nc.tensor.matmul_mx(
                        out=acc[t][:],
                        lhsT=x_codes[:, TOKENS * g : TOKENS * (g + 1)].bitcast(FP8X4),
                        lhsT_scale=x_scales[:, TOKENS * g : TOKENS * (g + 1)],
                        rhs=(
                            whole[g][:, N_TILE * t : N_TILE * (t + 1)]
                            if g < WHOLE
                            else words[r][g - WHOLE][:, N_TILE * i : N_TILE * (i + 1)]
                        ).bitcast(FP8X4),
                        rhs_scale=planes[k:P, c0 : c0 + N_TILE],
                        start=(g == 0),
                        stop=(g == GROUPS - 1),
                    )
            for t in tiles:
                if t == SHORT:
                    nc.scalar.copy(out=rows[t][:], in_=acc[t][:])
                    continue
                first[t] = turn.tile([P, N_TILE], F32, align_bytes=64, tag="first", name="first%d" % t)
                nc.vector.transpose(out=first[t][:], in_=acc[t][:])
                resorted[t] = turn.tile([P, N_TILE], F32, align_bytes=64, tag="sorted", name="sorted%d" % t)
                by_b = first[t][:].rearrange("p (h m l b) -> p b l m h", h=8, m=8, l=4, b=2)
                for b in (1, 0):
                    dst = resorted[t][:, 256 * b : 256 * (b + 1)].rearrange("p (l m h) -> p l m h", l=4, m=8)
                    if b == 1 or r == len(ROUNDS) - 1:
                        nc.vector.tensor_copy(out=dst, in_=by_b[:, b])
                    else:
                        nc.scalar.copy(out=dst, in_=by_b[:, b])
            for t in tiles:
                if t == SHORT:
                    continue
                for b in (1, 0):
                    half_cols = slice(256 * b, 256 * (b + 1))
                    nc.vector.transpose(out=rows[t][:, half_cols], in_=resorted[t][:, half_cols])

        for t in (0, 1, 2, 3, 4, 5, 6, 8, 7):
            o, part = divmod(t, TILES_PER_OUT)
            if t == SHORT:
                for b in (1, 0):
                    nc.sync.dma_start(
                        out=outs[o][b, HEADS_PER_TILE * part : HEADS_PER_TILE * (part + 1), :, :].rearrange("h n d -> n h d"),
                        in_=rows[t][b:P:2, :].rearrange("p (h d) -> p h d", h=HEADS_PER_TILE),
                    )
                continue
            for b in (1, 0):
                nc.sync.dma_start(
                    out=outs[o][b, HEADS_PER_TILE * part : HEADS_PER_TILE * (part + 1), :, :].rearrange(
                        "h (nh l) d -> nh h (l d)", l=4
                    ),
                    in_=rows[t][:, 256 * b : 256 * (b + 1)],
                )
